import numpy as np
import ml_dtypes


def mxq(x, axis, fmt="e4m3"):
    dtype, down = {"e4m3": (ml_dtypes.float8_e4m3fn, 7), "e5m2": (ml_dtypes.float8_e5m2, 14)}[fmt]
    v = np.moveaxis(np.asarray(x, np.float32).astype(ml_dtypes.bfloat16).astype(np.float64), axis, -1)
    blocks = v.reshape(v.shape[:-1] + (-1, 32))
    amax = np.abs(blocks).max(-1, keepdims=True)
    byte = np.maximum(np.where(amax > 0, np.frexp(amax)[1] - 1 + 127, 0) - down, 1)
    scale = np.exp2(byte - 127.0)
    codes = (blocks / scale).astype(np.float32).astype(dtype).astype(np.float64)
    return np.moveaxis((codes * scale).reshape(v.shape), -1, axis)


WIDE = False


def mx_kscale(k):
    if not WIDE:
        return np.ones(k)
    levels = np.array([10, -10, 5, -5, 0])
    a = np.random.permutation(np.resize(levels, k // 512 * 4)).reshape(k // 512, 4)
    idx = np.arange(k)
    return np.exp2(a[idx // 512, idx % 128 // 32])


BF16 = ml_dtypes.bfloat16


def bf(x):
    return np.asarray(x, np.float32).astype(BF16)


def f64(x):
    return np.asarray(x).astype(np.float64)


B, C, H, W, RQ, RV = 2, 1024, 64, 64, 4, 4
DQ, DV = C // RQ, C // RV
N = H * W


def maxpool2(x):
    b, c, h, w = x.shape
    return x.reshape(b, c, h // 2, 2, w // 2, 2).max(axis=(3, 5))


def setup_inputs():
    s = mx_kscale(C)
    return {"imgs": bf(np.random.standard_normal((B, C, H, W)) * s[None, :, None, None]),
            "w_kv": bf(np.random.standard_normal((DQ + DV, C)) * 0.5 / np.sqrt(C) / s[None, :])}


def reference(imgs, w_kv):
    x = f64(imgs).reshape(B, C, N)
    kv = (mxq(f64(w_kv), 1, "e4m3") @ mxq(x, 1, "e4m3")).reshape(B, DQ + DV, H, W)
    return maxpool2(kv[:, :DQ]), maxpool2(kv[:, DQ:])

@@ -1,0 +1,165 @@
+from contextlib import ExitStack
+
+import concourse.mybir as mybir
+from concourse.masks import make_identity
+
+BF16 = mybir.dt.bfloat16
+F32 = mybir.dt.float32
+U32 = mybir.dt.uint32
+U8 = mybir.dt.uint8
+FP8X4 = mybir.dt.float8_e4m3fn_x4
+
+IMAGES = 2
+CHANNELS = 1024
+SIDE = 64
+PIXELS = SIDE * SIDE
+OUTPUTS = 512
+
+P = 128
+PACK = 4
+K_PASS = P * PACK
+PASSES = CHANNELS // K_PASS
+M_TILES = OUTPUTS // P
+N_TILE = 512
+TILES_PER_IMAGE = PIXELS // N_TILE
+N_TILES = IMAGES * TILES_PER_IMAGE
+POOLED_TILE = N_TILE // 4
+FINE_TILES = 4
+LOAD_TILES = 2
+STORE_TILES = 2
+HEAD_TILES = 2
+HELPER_COLS = 256
+
+FLOPS = 2 * OUTPUTS * CHANNELS * IMAGES * PIXELS
+
+
+def tile_selfattentionconv2d_pa_t_kernel(tc, imgs, w_kv, out_0, out_1):
+    nc = tc.nc
+    with ExitStack() as ctx:
+        const = ctx.enter_context(tc.tile_pool(name="const", bufs=1))
+        raw_pool = ctx.enter_context(tc.tile_pool(name="raw", bufs=1))
+        grouped_pool = ctx.enter_context(tc.tile_pool(name="grouped", bufs=3))
+        codes_pool = ctx.enter_context(tc.tile_pool(name="codes", bufs=3))
+        pooled_pool = ctx.enter_context(tc.tile_pool(name="pooled", bufs=4))
+        psum = ctx.enter_context(tc.psum_pool(name="psum", bufs=8))
+        ctx.enter_context(tc.manual_schedule())
+
+        ident = const.tile([P, P], F32)
+        make_identity(nc, ident[:])
+
+        w_rows = []
+        for m in range(M_TILES):
+            w_rows.append(const.tile([P, CHANNELS], BF16, name="w_rows_%d" % m))
+            nc.sync.dma_start(out=w_rows[m][:], in_=w_kv[m * P : (m + 1) * P, :])
+        imgs_view = imgs.rearrange("b (g p t) h w -> b g p t (h w)", g=PASSES, p=P, t=PACK)
+        raw = {}
+        first = 0
+        while first < N_TILES:
+            count = 1 if first < FINE_TILES else LOAD_TILES
+            b, tile_in_image = divmod(first, TILES_PER_IMAGE)
+            for g in range(PASSES):
+                raw_tile = raw_pool.tile([P, PACK, count * N_TILE], BF16, name="raw_%d_%d" % (first, g))
+                nc.sync.dma_start(
+                    out=raw_tile[:],
+                    in_=imgs_view[b, g, :, :, tile_in_image * N_TILE : (tile_in_image + count) * N_TILE],
+                )
+                for k in range(count):
+                    raw[(first + k, g)] = raw_tile[:, :, k * N_TILE : (k + 1) * N_TILE]
+            first += count
+
+        w_grouped = const.tile([P, PASSES * M_TILES * P * PACK], BF16, align_bytes=64)
+        w_grouped_words = w_grouped[:].bitcast(F32).rearrange("p (g m o u) -> p m g o u", g=PASSES, m=M_TILES, u=2)
+        for m in range(M_TILES):
+            w_words = w_rows[m][:].bitcast(F32).rearrange("p (g q u) -> p g u q", g=PASSES, u=2)
+            w_t = psum.tile([P, N_TILE], F32, tag="bank", name="w_t")
+            for g in range(PASSES):
+                for u in range(2):
+                    nc.tensor.transpose(w_t[:, (2 * g + u) * P : (2 * g + u + 1) * P], w_words[:, g, u, :], ident[:])
+            nc.scalar.copy(out=w_grouped_words[:, m], in_=w_t[:].rearrange("p (g u o) -> p g o u", g=PASSES, u=2))
+        w_codes = const.tile([P, PASSES * M_TILES * P], U32, align_bytes=64)
+        w_scales = const.tile([P, PASSES * M_TILES * P], U8, align_bytes=64)
+        nc.vector.quantize_mx(out=w_codes[:].bitcast(FP8X4), scales=w_scales[:], in_=w_grouped[:])
+
+        grouped = {}
+        x_codes = {}
+        x_scales = {}
+        acc = {}
+        pooled = {}
+        out_views = [
+            out_0.rearrange("b (m p) i j -> b p m (i j)", p=P),
+            out_1.rearrange("b (m p) i j -> b p m (i j)", p=P),
+        ]
+
+        def regroup(n):
+            grouped[n] = grouped_pool.tile([P, PASSES, N_TILE, PACK], BF16, align_bytes=64, name="grouped")
+            for g in range(PASSES):
+                scalar_cols = N_TILE if g < PASSES - 1 else N_TILE - HELPER_COLS
+                dst = grouped[n][:, g, :scalar_cols, :].rearrange("p (c i) t -> p c t i", i=4)
+                src = raw[(n, g)][:, :, :scalar_cols].rearrange("p t (c i) -> p c t i", i=4)
+                if g == PASSES - 1 and n < HEAD_TILES:
+                    nc.vector.tensor_copy(out=dst, in_=src)
+                else:
+                    nc.scalar.copy(out=dst, in_=src)
+            nc.gpsimd.tensor_scalar(
+                out=grouped[n][:, PASSES - 1, N_TILE - HELPER_COLS :, :],
+                in0=raw[(n, PASSES - 1)][:, :, N_TILE - HELPER_COLS :].rearrange("p t w -> p w t"),
+                scalar1=1.0,
+                scalar2=0.0,
+                op0=mybir.AluOpType.mult,
+                op1=mybir.AluOpType.add,
+            )
+
+        def quantise(n):
+            x_codes[n] = codes_pool.tile([P, PASSES, N_TILE], U32, align_bytes=64, name="x_codes")
+            x_scales[n] = codes_pool.tile([P, PASSES, N_TILE], U8, align_bytes=64, name="x_scales")
+            nc.vector.quantize_mx(
+                out=x_codes[n][:].rearrange("p g w -> p (g w)").bitcast(FP8X4),
+                scales=x_scales[n][:].rearrange("p g w -> p (g w)"),
+                in_=grouped[n][:].rearrange("p g w t -> p (g w t)"),
+            )
+
+        def multiply(n):
+            for m in range(M_TILES):
+                acc[(n, m)] = psum.tile([P, N_TILE], F32, tag="bank", name="acc")
+                for g in range(PASSES):
+                    w_cols = slice((g * M_TILES + m) * P, (g * M_TILES + m + 1) * P)
+                    nc.tensor.matmul_mx(
+                        out=acc[(n, m)][:],
+                        lhsT=w_codes[:, w_cols].bitcast(FP8X4),
+                        lhsT_scale=w_scales[:, w_cols],
+                        rhs=x_codes[n][:, g, :].bitcast(FP8X4),
+                        rhs_scale=x_scales[n][:, g, :],
+                        start=(g == 0),
+                        stop=(g == PASSES - 1),
+                    )
+
+        def pool_and_store(n):
+            group, place = divmod(n, STORE_TILES)
+            b, group_in_image = divmod(group, TILES_PER_IMAGE // STORE_TILES)
+            store_cols = STORE_TILES * POOLED_TILE
+            if place == 0:
+                pooled[group] = pooled_pool.tile([P, M_TILES, store_cols], F32, name="pooled")
+            for m in range(M_TILES):
+                nc.vector.tensor_reduce(
+                    out=pooled[group][:, m, place * POOLED_TILE : (place + 1) * POOLED_TILE].rearrange(
+                        "p (i j) -> p i j", j=SIDE // 2
+                    ),
+                    in_=acc[(n, m)][:].rearrange("p (i di j dj) -> p i j di dj", di=2, j=SIDE // 2, dj=2),
+                    axis=mybir.AxisListType.XY,
+                    op=mybir.AluOpType.max,
+                )
+                if place == STORE_TILES - 1 and m % 2 == 1:
+                    nc.sync.dma_start(
+                        out=out_views[m // 2][b, :, :, group_in_image * store_cols : (group_in_image + 1) * store_cols],
+                        in_=pooled[group][:, m - 1 : m + 1, :],
+                    )
+
+        regroup(0)
+        for n in range(N_TILES):
+            quantise(n)
+            multiply(n)
+            if n + 1 < N_TILES:
+                regroup(n + 1)
+            if n >= 1:
+                pool_and_store(n - 1)
+        pool_and_store(N_TILES - 1)

@@ -28,7 +28,7 @@ FINE_TILES = 4
 LOAD_TILES = 2
 STORE_TILES = 2
 HEAD_TILES = 2
-HELPER_COLS = 256
+HELPER_COLS = 128
 
 FLOPS = 2 * OUTPUTS * CHANNELS * IMAGES * PIXELS
 
@@ -100,13 +100,9 @@ def tile_selfattentionconv2d_pa_t_kernel(tc, imgs, w_kv, out_0, out_1):
                     nc.vector.tensor_copy(out=dst, in_=src)
                 else:
                     nc.scalar.copy(out=dst, in_=src)
-            nc.gpsimd.tensor_scalar(
-                out=grouped[n][:, PASSES - 1, N_TILE - HELPER_COLS :, :],
-                in0=raw[(n, PASSES - 1)][:, :, N_TILE - HELPER_COLS :].rearrange("p t w -> p w t"),
-                scalar1=1.0,
-                scalar2=0.0,
-                op0=mybir.AluOpType.mult,
-                op1=mybir.AluOpType.add,
+            nc.vector.tensor_copy(
+                out=grouped[n][:, PASSES - 1, N_TILE - HELPER_COLS :, :].rearrange("p (c i) t -> p c t i", i=4),
+                in_=raw[(n, PASSES - 1)][:, :, N_TILE - HELPER_COLS :].rearrange("p t (c i) -> p c t i", i=4),
             )
 
         def quantise(n):

@@ -28,7 +28,7 @@ FINE_TILES = 4
 LOAD_TILES = 2
 STORE_TILES = 2
 HEAD_TILES = 2
-HELPER_COLS = 128
+HELPER_COLS = 192
 
 FLOPS = 2 * OUTPUTS * CHANNELS * IMAGES * PIXELS
 
@@ -75,7 +75,7 @@ def tile_selfattentionconv2d_pa_t_kernel(tc, imgs, w_kv, out_0, out_1):
             for g in range(PASSES):
                 for u in range(2):
                     nc.tensor.transpose(w_t[:, (2 * g + u) * P : (2 * g + u + 1) * P], w_words[:, g, u, :], ident[:])
-            nc.scalar.copy(out=w_grouped_words[:, m], in_=w_t[:].rearrange("p (g u o) -> p g o u", g=PASSES, u=2))
+            nc.vector.tensor_copy(out=w_grouped_words[:, m], in_=w_t[:].rearrange("p (g u o) -> p g o u", g=PASSES, u=2))
         w_codes = const.tile([P, PASSES * M_TILES * P], U32, align_bytes=64)
         w_scales = const.tile([P, PASSES * M_TILES * P], U8, align_bytes=64)
         nc.vector.quantize_mx(out=w_codes[:].bitcast(FP8X4), scales=w_scales[:], in_=w_grouped[:])
@@ -100,9 +100,13 @@ def tile_selfattentionconv2d_pa_t_kernel(tc, imgs, w_kv, out_0, out_1):
                     nc.vector.tensor_copy(out=dst, in_=src)
                 else:
                     nc.scalar.copy(out=dst, in_=src)
-            nc.vector.tensor_copy(
-                out=grouped[n][:, PASSES - 1, N_TILE - HELPER_COLS :, :].rearrange("p (c i) t -> p c t i", i=4),
-                in_=raw[(n, PASSES - 1)][:, :, N_TILE - HELPER_COLS :].rearrange("p t (c i) -> p c t i", i=4),
+            nc.gpsimd.tensor_scalar(
+                out=grouped[n][:, PASSES - 1, N_TILE - HELPER_COLS :, :],
+                in0=raw[(n, PASSES - 1)][:, :, N_TILE - HELPER_COLS :].rearrange("p t w -> p w t"),
+                scalar1=1.0,
+                scalar2=0.0,
+                op0=mybir.AluOpType.mult,
+                op1=mybir.AluOpType.add,
             )
 
         def quantise(n):

@@ -28,7 +28,7 @@ FINE_TILES = 4
 LOAD_TILES = 2
 STORE_TILES = 2
 HEAD_TILES = 2
-HELPER_COLS = 192
+HELPER_COLS = 320
 
 FLOPS = 2 * OUTPUTS * CHANNELS * IMAGES * PIXELS
 

@@ -26,8 +26,11 @@ N_TILES = IMAGES * TILES_PER_IMAGE
 POOLED_TILE = N_TILE // 4
 FINE_TILES = 4
 LOAD_TILES = 2
+LOAD_AHEAD = 8
 STORE_TILES = 2
 HEAD_TILES = 2
+UNHELPED_TILES = 3
+FREE_TILES = 3
 HELPER_COLS = 320
 
 FLOPS = 2 * OUTPUTS * CHANNELS * IMAGES * PIXELS
@@ -41,6 +44,7 @@ def tile_selfattentionconv2d_pa_t_kernel(tc, imgs, w_kv, out_0, out_1):
         grouped_pool = ctx.enter_context(tc.tile_pool(name="grouped", bufs=3))
         codes_pool = ctx.enter_context(tc.tile_pool(name="codes", bufs=3))
         pooled_pool = ctx.enter_context(tc.tile_pool(name="pooled", bufs=4))
+        halves_pool = ctx.enter_context(tc.tile_pool(name="halves", bufs=2))
         psum = ctx.enter_context(tc.psum_pool(name="psum", bufs=8))
         ctx.enter_context(tc.manual_schedule())
 
@@ -53,9 +57,8 @@ def tile_selfattentionconv2d_pa_t_kernel(tc, imgs, w_kv, out_0, out_1):
             nc.sync.dma_start(out=w_rows[m][:], in_=w_kv[m * P : (m + 1) * P, :])
         imgs_view = imgs.rearrange("b (g p t) h w -> b g p t (h w)", g=PASSES, p=P, t=PACK)
         raw = {}
-        first = 0
-        while first < N_TILES:
-            count = 1 if first < FINE_TILES else LOAD_TILES
+
+        def load(first, count):
             b, tile_in_image = divmod(first, TILES_PER_IMAGE)
             for g in range(PASSES):
                 raw_tile = raw_pool.tile([P, PACK, count * N_TILE], BF16, name="raw_%d_%d" % (first, g))
@@ -65,7 +68,11 @@ def tile_selfattentionconv2d_pa_t_kernel(tc, imgs, w_kv, out_0, out_1):
                 )
                 for k in range(count):
                     raw[(first + k, g)] = raw_tile[:, :, k * N_TILE : (k + 1) * N_TILE]
-            first += count
+
+        for first in range(FINE_TILES):
+            load(first, 1)
+        for first in range(FINE_TILES, LOAD_AHEAD, LOAD_TILES):
+            load(first, LOAD_TILES)
 
         w_grouped = const.tile([P, PASSES * M_TILES * P * PACK], BF16, align_bytes=64)
         w_grouped_words = w_grouped[:].bitcast(F32).rearrange("p (g m o u) -> p m g o u", g=PASSES, m=M_TILES, u=2)
@@ -85,6 +92,7 @@ def tile_selfattentionconv2d_pa_t_kernel(tc, imgs, w_kv, out_0, out_1):
         x_scales = {}
         acc = {}
         pooled = {}
+        odd_rows = {}
         out_views = [
             out_0.rearrange("b (m p) i j -> b p m (i j)", p=P),
             out_1.rearrange("b (m p) i j -> b p m (i j)", p=P),
@@ -133,26 +141,76 @@ def tile_selfattentionconv2d_pa_t_kernel(tc, imgs, w_kv, out_0, out_1):
                         stop=(g == PASSES - 1),
                     )
 
+        def helped(n):
+            if n < UNHELPED_TILES:
+                return 0
+            if n == N_TILES - 1:
+                return M_TILES // 2
+            return M_TILES if n >= N_TILES - FREE_TILES else 1
+
+        def copy_odd_rows(n):
+            odd_rows[n] = halves_pool.tile([P, M_TILES, N_TILE // 2], F32, name="odd_rows")
+            for m in range(helped(n)):
+                nc.scalar.copy(
+                    out=odd_rows[n][:, m, :].rearrange("p (i x) -> p i x", x=SIDE),
+                    in_=acc[(n, m)][:].rearrange("p (i di x) -> p i di x", di=2, x=SIDE)[:, :, 1, :],
+                )
+
         def pool_and_store(n):
             group, place = divmod(n, STORE_TILES)
             b, group_in_image = divmod(group, TILES_PER_IMAGE // STORE_TILES)
             store_cols = STORE_TILES * POOLED_TILE
+            cols = slice(place * POOLED_TILE, (place + 1) * POOLED_TILE)
             if place == 0:
                 pooled[group] = pooled_pool.tile([P, M_TILES, store_cols], F32, name="pooled")
-            for m in range(M_TILES):
-                nc.vector.tensor_reduce(
-                    out=pooled[group][:, m, place * POOLED_TILE : (place + 1) * POOLED_TILE].rearrange(
-                        "p (i j) -> p i j", j=SIDE // 2
-                    ),
-                    in_=acc[(n, m)][:].rearrange("p (i di j dj) -> p i j di dj", di=2, j=SIDE // 2, dj=2),
-                    axis=mybir.AxisListType.XY,
-                    op=mybir.AluOpType.max,
-                )
-                if place == STORE_TILES - 1 and m % 2 == 1:
-                    nc.sync.dma_start(
-                        out=out_views[m // 2][b, :, :, group_in_image * store_cols : (group_in_image + 1) * store_cols],
-                        in_=pooled[group][:, m - 1 : m + 1, :],
+            row_max = halves_pool.tile([P, M_TILES, N_TILE // 2], F32, name="row_max")
+
+            def rows_step():
+                for m in range(helped(n)):
+                    nc.vector.tensor_tensor(
+                        out=row_max[:, m, :].rearrange("p (i x) -> p i x", x=SIDE),
+                        in0=acc[(n, m)][:].rearrange("p (i di x) -> p i di x", di=2, x=SIDE)[:, :, 0, :],
+                        in1=odd_rows[n][:, m, :].rearrange("p (i x) -> p i x", x=SIDE),
+                        op=mybir.AluOpType.max,
                     )
+
+            def columns_step():
+                if helped(n) > 0:
+                    pairs = row_max[:, : helped(n), :].rearrange("p m (o dj) -> p m o dj", dj=2)
+                    nc.vector.tensor_tensor(
+                        out=pooled[group][:, : helped(n), cols],
+                        in0=pairs[:, :, :, 0],
+                        in1=pairs[:, :, :, 1],
+                        op=mybir.AluOpType.max,
+                    )
+
+            def reduces():
+                for m in range(helped(n), M_TILES):
+                    nc.vector.tensor_reduce(
+                        out=pooled[group][:, m, cols].rearrange("p (i j) -> p i j", j=SIDE // 2),
+                        in_=acc[(n, m)][:].rearrange("p (i di j dj) -> p i j di dj", di=2, j=SIDE // 2, dj=2),
+                        axis=mybir.AxisListType.XY,
+                        op=mybir.AluOpType.max,
+                    )
+
+            def store(half):
+                if place == STORE_TILES - 1:
+                    nc.sync.dma_start(
+                        out=out_views[half][b, :, :, group_in_image * store_cols : (group_in_image + 1) * store_cols],
+                        in_=pooled[group][:, 2 * half : 2 * half + 2, :],
+                    )
+
+            rows_step()
+            if n == N_TILES - 1:
+                columns_step()
+                store(0)
+                reduces()
+                store(1)
+            else:
+                reduces()
+                columns_step()
+                store(0)
+                store(1)
 
         regroup(0)
         for n in range(N_TILES):
@@ -161,5 +219,9 @@ def tile_selfattentionconv2d_pa_t_kernel(tc, imgs, w_kv, out_0, out_1):
             if n + 1 < N_TILES:
                 regroup(n + 1)
             if n >= 1:
+                copy_odd_rows(n - 1)
                 pool_and_store(n - 1)
+            if n % LOAD_TILES == 0 and LOAD_TILES <= n and n + LOAD_AHEAD - LOAD_TILES < N_TILES:
+                load(n + LOAD_AHEAD - LOAD_TILES, LOAD_TILES)
+        copy_odd_rows(N_TILES - 1)
         pool_and_store(N_TILES - 1)

@@ -185,7 +185,10 @@ def tile_selfattentionconv2d_pa_t_kernel(tc, imgs, w_kv, out_0, out_1):
                     )
 
             def reduces():
-                for m in range(helped(n), M_TILES):
+                banks = list(range(helped(n), M_TILES))
+                if n < N_TILES - 1:
+                    banks = list(reversed(banks))
+                for m in banks:
                     nc.vector.tensor_reduce(
                         out=pooled[group][:, m, cols].rearrange("p (i j) -> p i j", j=SIDE // 2),
                         in_=acc[(n, m)][:].rearrange("p (i di j dj) -> p i j di dj", di=2, j=SIDE // 2, dj=2),

@@ -186,7 +186,7 @@ def tile_selfattentionconv2d_pa_t_kernel(tc, imgs, w_kv, out_0, out_1):
 
             def reduces():
                 banks = list(range(helped(n), M_TILES))
-                if n < N_TILES - 1:
+                if UNHELPED_TILES <= n < N_TILES - 1:
                     banks = list(reversed(banks))
                 for m in banks:
                     nc.vector.tensor_reduce(

@@ -29,6 +29,7 @@ LOAD_TILES = 2
 LOAD_AHEAD = 8
 STORE_TILES = 2
 HEAD_TILES = 2
+SINGLE_TILES = 4
 UNHELPED_TILES = 3
 FREE_TILES = 3
 HELPER_COLS = 320
@@ -93,6 +94,7 @@ def tile_selfattentionconv2d_pa_t_kernel(tc, imgs, w_kv, out_0, out_1):
         acc = {}
         pooled = {}
         odd_rows = {}
+        row_max = {}
         out_views = [
             out_0.rearrange("b (m p) i j -> b p m (i j)", p=P),
             out_1.rearrange("b (m p) i j -> b p m (i j)", p=P),
@@ -156,75 +158,104 @@ def tile_selfattentionconv2d_pa_t_kernel(tc, imgs, w_kv, out_0, out_1):
                     in_=acc[(n, m)][:].rearrange("p (i di x) -> p i di x", di=2, x=SIDE)[:, :, 1, :],
                 )
 
-        def pool_and_store(n):
+        def place_of(n):
             group, place = divmod(n, STORE_TILES)
             b, group_in_image = divmod(group, TILES_PER_IMAGE // STORE_TILES)
+            return group, place, b, group_in_image
+
+        def pooled_cols(n):
+            place = place_of(n)[1]
+            return slice(place * POOLED_TILE, (place + 1) * POOLED_TILE)
+
+        def rows_step(n):
+            row_max[n] = halves_pool.tile([P, M_TILES, N_TILE // 2], F32, name="row_max")
+            for m in range(helped(n)):
+                nc.vector.tensor_tensor(
+                    out=row_max[n][:, m, :].rearrange("p (i x) -> p i x", x=SIDE),
+                    in0=acc[(n, m)][:].rearrange("p (i di x) -> p i di x", di=2, x=SIDE)[:, :, 0, :],
+                    in1=odd_rows[n][:, m, :].rearrange("p (i x) -> p i x", x=SIDE),
+                    op=mybir.AluOpType.max,
+                )
+
+        def reduces(n):
+            group = place_of(n)[0]
+            for m in range(helped(n), M_TILES):
+                nc.vector.tensor_reduce(
+                    out=pooled[group][:, m, pooled_cols(n)].rearrange("p (i j) -> p i j", j=SIDE // 2),
+                    in_=acc[(n, m)][:].rearrange("p (i di j dj) -> p i j di dj", di=2, j=SIDE // 2, dj=2),
+                    axis=mybir.AxisListType.XY,
+                    op=mybir.AluOpType.max,
+                )
+
+        def columns_step(n):
+            group = place_of(n)[0]
+            if helped(n) > 0:
+                pairs = row_max[n][:, : helped(n), :].rearrange("p m (o dj) -> p m o dj", dj=2)
+                nc.vector.tensor_tensor(
+                    out=pooled[group][:, : helped(n), pooled_cols(n)],
+                    in0=pairs[:, :, :, 0],
+                    in1=pairs[:, :, :, 1],
+                    op=mybir.AluOpType.max,
+                )
+
+        def store(n, half):
+            group, place, b, group_in_image = place_of(n)
             store_cols = STORE_TILES * POOLED_TILE
-            cols = slice(place * POOLED_TILE, (place + 1) * POOLED_TILE)
+            if place == STORE_TILES - 1:
+                nc.sync.dma_start(
+                    out=out_views[half][b, :, :, group_in_image * store_cols : (group_in_image + 1) * store_cols],
+                    in_=pooled[group][:, 2 * half : 2 * half + 2, :],
+                )
+
+        def empty_banks(n):
+            group, place = place_of(n)[:2]
             if place == 0:
-                pooled[group] = pooled_pool.tile([P, M_TILES, store_cols], F32, name="pooled")
-            row_max = halves_pool.tile([P, M_TILES, N_TILE // 2], F32, name="row_max")
+                pooled[group] = pooled_pool.tile([P, M_TILES, STORE_TILES * POOLED_TILE], F32, name="pooled")
+            rows_step(n)
+            reduces(n)
 
-            def rows_step():
-                for m in range(helped(n)):
-                    nc.vector.tensor_tensor(
-                        out=row_max[:, m, :].rearrange("p (i x) -> p i x", x=SIDE),
-                        in0=acc[(n, m)][:].rearrange("p (i di x) -> p i di x", di=2, x=SIDE)[:, :, 0, :],
-                        in1=odd_rows[n][:, m, :].rearrange("p (i x) -> p i x", x=SIDE),
-                        op=mybir.AluOpType.max,
-                    )
+        def finish(n):
+            columns_step(n)
+            store(n, 0)
+            store(n, 1)
 
-            def columns_step():
-                if helped(n) > 0:
-                    pairs = row_max[:, : helped(n), :].rearrange("p m (o dj) -> p m o dj", dj=2)
-                    nc.vector.tensor_tensor(
-                        out=pooled[group][:, : helped(n), cols],
-                        in0=pairs[:, :, :, 0],
-                        in1=pairs[:, :, :, 1],
-                        op=mybir.AluOpType.max,
-                    )
-
-            def reduces():
-                banks = list(range(helped(n), M_TILES))
-                if UNHELPED_TILES <= n < N_TILES - 1:
-                    banks = list(reversed(banks))
-                for m in banks:
-                    nc.vector.tensor_reduce(
-                        out=pooled[group][:, m, cols].rearrange("p (i j) -> p i j", j=SIDE // 2),
-                        in_=acc[(n, m)][:].rearrange("p (i di j dj) -> p i j di dj", di=2, j=SIDE // 2, dj=2),
-                        axis=mybir.AxisListType.XY,
-                        op=mybir.AluOpType.max,
-                    )
-
-            def store(half):
-                if place == STORE_TILES - 1:
-                    nc.sync.dma_start(
-                        out=out_views[half][b, :, :, group_in_image * store_cols : (group_in_image + 1) * store_cols],
-                        in_=pooled[group][:, 2 * half : 2 * half + 2, :],
-                    )
-
-            rows_step()
-            if n == N_TILES - 1:
-                columns_step()
-                store(0)
-                reduces()
-                store(1)
-            else:
-                reduces()
-                columns_step()
-                store(0)
-                store(1)
+        def load_behind_stores(n):
+            if LOAD_TILES <= n and n + LOAD_AHEAD - LOAD_TILES < N_TILES:
+                load(n + LOAD_AHEAD - LOAD_TILES, LOAD_TILES)
 
         regroup(0)
-        for n in range(N_TILES):
+        for n in range(SINGLE_TILES):
             quantise(n)
             multiply(n)
-            if n + 1 < N_TILES:
-                regroup(n + 1)
+            regroup(n + 1)
+            if n == SINGLE_TILES - 1:
+                regroup(n + 2)
             if n >= 1:
                 copy_odd_rows(n - 1)
-                pool_and_store(n - 1)
-            if n % LOAD_TILES == 0 and LOAD_TILES <= n and n + LOAD_AHEAD - LOAD_TILES < N_TILES:
-                load(n + LOAD_AHEAD - LOAD_TILES, LOAD_TILES)
-        copy_odd_rows(N_TILES - 1)
-        pool_and_store(N_TILES - 1)
+                empty_banks(n - 1)
+                finish(n - 1)
+            if n % LOAD_TILES == 0:
+                load_behind_stores(n)
+        for a in range(SINGLE_TILES, N_TILES, 2):
+            quantise(a)
+            multiply(a)
+            quantise(a + 1)
+            copy_odd_rows(a - 1)
+            if a + 2 < N_TILES:
+                regroup(a + 2)
+            empty_banks(a - 1)
+            multiply(a + 1)
+            copy_odd_rows(a)
+            if a + 3 < N_TILES:
+                regroup(a + 3)
+            empty_banks(a)
+            finish(a - 1)
+            finish(a)
+            load_behind_stores(a)
+        last = N_TILES - 1
+        copy_odd_rows(last)
+        rows_step(last)
+        columns_step(last)
+        store(last, 0)
+        reduces(last)
+        store(last, 1)

@@ -28,6 +28,7 @@ FINE_TILES = 4
 LOAD_TILES = 2
 LOAD_AHEAD = 8
 STORE_TILES = 2
+HEAD_HELPER_COLS = 192
 HEAD_TILES = 2
 SINGLE_TILES = 4
 UNHELPED_TILES = 3
@@ -76,17 +77,26 @@ def tile_selfattentionconv2d_pa_t_kernel(tc, imgs, w_kv, out_0, out_1):
             load(first, LOAD_TILES)
 
         w_grouped = const.tile([P, PASSES * M_TILES * P * PACK], BF16, align_bytes=64)
-        w_grouped_words = w_grouped[:].bitcast(F32).rearrange("p (g m o u) -> p m g o u", g=PASSES, m=M_TILES, u=2)
+        w_grouped_words = w_grouped[:].bitcast(F32).rearrange("p (m g o u) -> p m g o u", g=PASSES, m=M_TILES, u=2)
         for m in range(M_TILES):
             w_words = w_rows[m][:].bitcast(F32).rearrange("p (g q u) -> p g u q", g=PASSES, u=2)
             w_t = psum.tile([P, N_TILE], F32, tag="bank", name="w_t")
             for g in range(PASSES):
                 for u in range(2):
                     nc.tensor.transpose(w_t[:, (2 * g + u) * P : (2 * g + u + 1) * P], w_words[:, g, u, :], ident[:])
-            nc.vector.tensor_copy(out=w_grouped_words[:, m], in_=w_t[:].rearrange("p (g u o) -> p g o u", g=PASSES, u=2))
-        w_codes = const.tile([P, PASSES * M_TILES * P], U32, align_bytes=64)
-        w_scales = const.tile([P, PASSES * M_TILES * P], U8, align_bytes=64)
-        nc.vector.quantize_mx(out=w_codes[:].bitcast(FP8X4), scales=w_scales[:], in_=w_grouped[:])
+            if m % 2 == 0:
+                nc.vector.tensor_copy(out=w_grouped_words[:, m], in_=w_t[:].rearrange("p (g u o) -> p g o u", g=PASSES, u=2))
+            else:
+                nc.scalar.copy(out=w_grouped_words[:, m], in_=w_t[:].rearrange("p (g u o) -> p g o u", g=PASSES, u=2))
+        w_codes = const.tile([P, M_TILES * PASSES * P], U32, align_bytes=64)
+        w_scales = const.tile([P, M_TILES * PASSES * P], U8, align_bytes=64)
+        half = M_TILES * PASSES * P // 2
+        for k in range(2):
+            nc.vector.quantize_mx(
+                out=w_codes[:, k * half : (k + 1) * half].bitcast(FP8X4),
+                scales=w_scales[:, k * half : (k + 1) * half],
+                in_=w_grouped[:, k * half * PACK : (k + 1) * half * PACK],
+            )
 
         grouped = {}
         x_codes = {}
@@ -102,22 +112,25 @@ def tile_selfattentionconv2d_pa_t_kernel(tc, imgs, w_kv, out_0, out_1):
 
         def regroup(n):
             grouped[n] = grouped_pool.tile([P, PASSES, N_TILE, PACK], BF16, align_bytes=64, name="grouped")
+            helper_cols = HEAD_HELPER_COLS if n < HEAD_TILES else HELPER_COLS
             for g in range(PASSES):
-                scalar_cols = N_TILE if g < PASSES - 1 else N_TILE - HELPER_COLS
-                dst = grouped[n][:, g, :scalar_cols, :].rearrange("p (c i) t -> p c t i", i=4)
-                src = raw[(n, g)][:, :, :scalar_cols].rearrange("p t (c i) -> p c t i", i=4)
+                helper_here = g == PASSES - 1 or n == 0
+                cols = N_TILE - helper_cols if helper_here else N_TILE
+                dst = grouped[n][:, g, :cols, :].rearrange("p (c i) t -> p c t i", i=4)
+                src = raw[(n, g)][:, :, :cols].rearrange("p t (c i) -> p c t i", i=4)
                 if g == PASSES - 1 and n < HEAD_TILES:
                     nc.vector.tensor_copy(out=dst, in_=src)
                 else:
                     nc.scalar.copy(out=dst, in_=src)
-            nc.gpsimd.tensor_scalar(
-                out=grouped[n][:, PASSES - 1, N_TILE - HELPER_COLS :, :],
-                in0=raw[(n, PASSES - 1)][:, :, N_TILE - HELPER_COLS :].rearrange("p t w -> p w t"),
-                scalar1=1.0,
-                scalar2=0.0,
-                op0=mybir.AluOpType.mult,
-                op1=mybir.AluOpType.add,
-            )
+                if helper_here:
+                    nc.gpsimd.tensor_scalar(
+                        out=grouped[n][:, g, cols:, :],
+                        in0=raw[(n, g)][:, :, cols:].rearrange("p t w -> p w t"),
+                        scalar1=1.0,
+                        scalar2=0.0,
+                        op0=mybir.AluOpType.mult,
+                        op1=mybir.AluOpType.add,
+                    )
 
         def quantise(n):
             x_codes[n] = codes_pool.tile([P, PASSES, N_TILE], U32, align_bytes=64, name="x_codes")
@@ -132,7 +145,7 @@ def tile_selfattentionconv2d_pa_t_kernel(tc, imgs, w_kv, out_0, out_1):
             for m in range(M_TILES):
                 acc[(n, m)] = psum.tile([P, N_TILE], F32, tag="bank", name="acc")
                 for g in range(PASSES):
-                    w_cols = slice((g * M_TILES + m) * P, (g * M_TILES + m + 1) * P)
+                    w_cols = slice((m * PASSES + g) * P, (m * PASSES + g + 1) * P)
                     nc.tensor.matmul_mx(
                         out=acc[(n, m)][:],
                         lhsT=w_codes[:, w_cols].bitcast(FP8X4),

@@ -26,7 +26,7 @@ N_TILES = IMAGES * TILES_PER_IMAGE
 POOLED_TILE = N_TILE // 4
 FINE_TILES = 4
 LOAD_TILES = 2
-LOAD_AHEAD = 8
+LOAD_AHEAD = 10
 STORE_TILES = 2
 HEAD_HELPER_COLS = 192
 HEAD_TILES = 2
@@ -104,13 +104,16 @@ def tile_selfattentionconv2d_pa_t_kernel(tc, imgs, w_kv, out_0, out_1):
         acc = {}
         pooled = {}
         odd_rows = {}
+        held = const.tile([P, 2], U32)
         row_max = {}
         out_views = [
             out_0.rearrange("b (m p) i j -> b p m (i j)", p=P),
             out_1.rearrange("b (m p) i j -> b p m (i j)", p=P),
         ]
 
-        def regroup(n):
+        def regroup(n, after=None):
+            if after is not None:
+                nc.gpsimd.tensor_copy(out=held[:], in_=x_codes[after][:, 0, :2])
             grouped[n] = grouped_pool.tile([P, PASSES, N_TILE, PACK], BF16, align_bytes=64, name="grouped")
             helper_cols = HEAD_HELPER_COLS if n < HEAD_TILES else HELPER_COLS
             for g in range(PASSES):
@@ -159,8 +162,6 @@ def tile_selfattentionconv2d_pa_t_kernel(tc, imgs, w_kv, out_0, out_1):
         def helped(n):
             if n < UNHELPED_TILES:
                 return 0
-            if n == N_TILES - 1:
-                return M_TILES // 2
             return M_TILES if n >= N_TILES - FREE_TILES else 1
 
         def copy_odd_rows(n):
@@ -200,12 +201,12 @@ def tile_selfattentionconv2d_pa_t_kernel(tc, imgs, w_kv, out_0, out_1):
                     op=mybir.AluOpType.max,
                 )
 
-        def columns_step(n):
+        def columns_step(n, first_bank, banks):
             group = place_of(n)[0]
-            if helped(n) > 0:
-                pairs = row_max[n][:, : helped(n), :].rearrange("p m (o dj) -> p m o dj", dj=2)
+            if banks > 0:
+                pairs = row_max[n][:, first_bank : first_bank + banks, :].rearrange("p m (o dj) -> p m o dj", dj=2)
                 nc.vector.tensor_tensor(
-                    out=pooled[group][:, : helped(n), pooled_cols(n)],
+                    out=pooled[group][:, first_bank : first_bank + banks, pooled_cols(n)],
                     in0=pairs[:, :, :, 0],
                     in1=pairs[:, :, :, 1],
                     op=mybir.AluOpType.max,
@@ -228,7 +229,7 @@ def tile_selfattentionconv2d_pa_t_kernel(tc, imgs, w_kv, out_0, out_1):
             reduces(n)
 
         def finish(n):
-            columns_step(n)
+            columns_step(n, 0, helped(n))
             store(n, 0)
             store(n, 1)
 
@@ -255,7 +256,7 @@ def tile_selfattentionconv2d_pa_t_kernel(tc, imgs, w_kv, out_0, out_1):
             quantise(a + 1)
             copy_odd_rows(a - 1)
             if a + 2 < N_TILES:
-                regroup(a + 2)
+                regroup(a + 2, after=a + 1)
             empty_banks(a - 1)
             multiply(a + 1)
             copy_odd_rows(a)
@@ -268,7 +269,6 @@ def tile_selfattentionconv2d_pa_t_kernel(tc, imgs, w_kv, out_0, out_1):
         last = N_TILES - 1
         copy_odd_rows(last)
         rows_step(last)
-        columns_step(last)
-        store(last, 0)
-        reduces(last)
-        store(last, 1)
+        for half in range(2):
+            columns_step(last, half * M_TILES // 2, M_TILES // 2)
+            store(last, half)

from contextlib import ExitStack

import concourse.mybir as mybir
from concourse.masks import make_identity

BF16 = mybir.dt.bfloat16
F32 = mybir.dt.float32
U32 = mybir.dt.uint32
U8 = mybir.dt.uint8
FP8X4 = mybir.dt.float8_e4m3fn_x4

IMAGES = 2
CHANNELS = 1024
SIDE = 64
PIXELS = SIDE * SIDE
OUTPUTS = 512

P = 128
PACK = 4
K_PASS = P * PACK
PASSES = CHANNELS // K_PASS
M_TILES = OUTPUTS // P
N_TILE = 512
TILES_PER_IMAGE = PIXELS // N_TILE
N_TILES = IMAGES * TILES_PER_IMAGE
POOLED_TILE = N_TILE // 4
FINE_TILES = 4
LOAD_TILES = 2
LOAD_AHEAD = 10
STORE_TILES = 2
HEAD_HELPER_COLS = 192
HEAD_TILES = 2
SINGLE_TILES = 4
UNHELPED_TILES = 3
FREE_TILES = 3
HELPER_COLS = 320

FLOPS = 2 * OUTPUTS * CHANNELS * IMAGES * PIXELS


def tile_selfattentionconv2d_pa_t_kernel(tc, imgs, w_kv, out_0, out_1):
    nc = tc.nc
    with ExitStack() as ctx:
        const = ctx.enter_context(tc.tile_pool(name="const", bufs=1))
        raw_pool = ctx.enter_context(tc.tile_pool(name="raw", bufs=1))
        grouped_pool = ctx.enter_context(tc.tile_pool(name="grouped", bufs=3))
        codes_pool = ctx.enter_context(tc.tile_pool(name="codes", bufs=3))
        pooled_pool = ctx.enter_context(tc.tile_pool(name="pooled", bufs=4))
        halves_pool = ctx.enter_context(tc.tile_pool(name="halves", bufs=2))
        psum = ctx.enter_context(tc.psum_pool(name="psum", bufs=8))
        ctx.enter_context(tc.manual_schedule())

        ident = const.tile([P, P], F32)
        make_identity(nc, ident[:])

        w_rows = []
        for m in range(M_TILES):
            w_rows.append(const.tile([P, CHANNELS], BF16, name="w_rows_%d" % m))
            nc.sync.dma_start(out=w_rows[m][:], in_=w_kv[m * P : (m + 1) * P, :])
        imgs_view = imgs.rearrange("b (g p t) h w -> b g p t (h w)", g=PASSES, p=P, t=PACK)
        raw = {}

        def load(first, count):
            b, tile_in_image = divmod(first, TILES_PER_IMAGE)
            for g in range(PASSES):
                raw_tile = raw_pool.tile([P, PACK, count * N_TILE], BF16, name="raw_%d_%d" % (first, g))
                nc.sync.dma_start(
                    out=raw_tile[:],
                    in_=imgs_view[b, g, :, :, tile_in_image * N_TILE : (tile_in_image + count) * N_TILE],
                )
                for k in range(count):
                    raw[(first + k, g)] = raw_tile[:, :, k * N_TILE : (k + 1) * N_TILE]

        for first in range(FINE_TILES):
            load(first, 1)
        for first in range(FINE_TILES, LOAD_AHEAD, LOAD_TILES):
            load(first, LOAD_TILES)

        w_grouped = const.tile([P, PASSES * M_TILES * P * PACK], BF16, align_bytes=64)
        w_grouped_words = w_grouped[:].bitcast(F32).rearrange("p (m g o u) -> p m g o u", g=PASSES, m=M_TILES, u=2)
        for m in range(M_TILES):
            w_words = w_rows[m][:].bitcast(F32).rearrange("p (g q u) -> p g u q", g=PASSES, u=2)
            w_t = psum.tile([P, N_TILE], F32, tag="bank", name="w_t")
            for g in range(PASSES):
                for u in range(2):
                    nc.tensor.transpose(w_t[:, (2 * g + u) * P : (2 * g + u + 1) * P], w_words[:, g, u, :], ident[:])
            if m % 2 == 0:
                nc.vector.tensor_copy(out=w_grouped_words[:, m], in_=w_t[:].rearrange("p (g u o) -> p g o u", g=PASSES, u=2))
            else:
                nc.scalar.copy(out=w_grouped_words[:, m], in_=w_t[:].rearrange("p (g u o) -> p g o u", g=PASSES, u=2))
        w_codes = const.tile([P, M_TILES * PASSES * P], U32, align_bytes=64)
        w_scales = const.tile([P, M_TILES * PASSES * P], U8, align_bytes=64)
        half = M_TILES * PASSES * P // 2
        for k in range(2):
            nc.vector.quantize_mx(
                out=w_codes[:, k * half : (k + 1) * half].bitcast(FP8X4),
                scales=w_scales[:, k * half : (k + 1) * half],
                in_=w_grouped[:, k * half * PACK : (k + 1) * half * PACK],
            )

        grouped = {}
        x_codes = {}
        x_scales = {}
        acc = {}
        pooled = {}
        odd_rows = {}
        held = const.tile([P, 2], U32)
        row_max = {}
        out_views = [
            out_0.rearrange("b (m p) i j -> b p m (i j)", p=P),
            out_1.rearrange("b (m p) i j -> b p m (i j)", p=P),
        ]

        def regroup(n, after=None):
            if after is not None:
                nc.gpsimd.tensor_copy(out=held[:], in_=x_codes[after][:, 0, :2])
            grouped[n] = grouped_pool.tile([P, PASSES, N_TILE, PACK], BF16, align_bytes=64, name="grouped")
            helper_cols = HEAD_HELPER_COLS if n < HEAD_TILES else HELPER_COLS
            for g in range(PASSES):
                helper_here = g == PASSES - 1 or n == 0
                cols = N_TILE - helper_cols if helper_here else N_TILE
                dst = grouped[n][:, g, :cols, :].rearrange("p (c i) t -> p c t i", i=4)
                src = raw[(n, g)][:, :, :cols].rearrange("p t (c i) -> p c t i", i=4)
                if g == PASSES - 1 and n < HEAD_TILES:
                    nc.vector.tensor_copy(out=dst, in_=src)
                else:
                    nc.scalar.copy(out=dst, in_=src)
                if helper_here:
                    nc.gpsimd.tensor_scalar(
                        out=grouped[n][:, g, cols:, :],
                        in0=raw[(n, g)][:, :, cols:].rearrange("p t w -> p w t"),
                        scalar1=1.0,
                        scalar2=0.0,
                        op0=mybir.AluOpType.mult,
                        op1=mybir.AluOpType.add,
                    )

        def quantise(n):
            x_codes[n] = codes_pool.tile([P, PASSES, N_TILE], U32, align_bytes=64, name="x_codes")
            x_scales[n] = codes_pool.tile([P, PASSES, N_TILE], U8, align_bytes=64, name="x_scales")
            nc.vector.quantize_mx(
                out=x_codes[n][:].rearrange("p g w -> p (g w)").bitcast(FP8X4),
                scales=x_scales[n][:].rearrange("p g w -> p (g w)"),
                in_=grouped[n][:].rearrange("p g w t -> p (g w t)"),
            )

        def multiply(n):
            for m in range(M_TILES):
                acc[(n, m)] = psum.tile([P, N_TILE], F32, tag="bank", name="acc")
                for g in range(PASSES):
                    w_cols = slice((m * PASSES + g) * P, (m * PASSES + g + 1) * P)
                    nc.tensor.matmul_mx(
                        out=acc[(n, m)][:],
                        lhsT=w_codes[:, w_cols].bitcast(FP8X4),
                        lhsT_scale=w_scales[:, w_cols],
                        rhs=x_codes[n][:, g, :].bitcast(FP8X4),
                        rhs_scale=x_scales[n][:, g, :],
                        start=(g == 0),
                        stop=(g == PASSES - 1),
                    )

        def helped(n):
            if n < UNHELPED_TILES:
                return 0
            return M_TILES if n >= N_TILES - FREE_TILES else 1

        def copy_odd_rows(n):
            odd_rows[n] = halves_pool.tile([P, M_TILES, N_TILE // 2], F32, name="odd_rows")
            for m in range(helped(n)):
                nc.scalar.copy(
                    out=odd_rows[n][:, m, :].rearrange("p (i x) -> p i x", x=SIDE),
                    in_=acc[(n, m)][:].rearrange("p (i di x) -> p i di x", di=2, x=SIDE)[:, :, 1, :],
                )

        def place_of(n):
            group, place = divmod(n, STORE_TILES)
            b, group_in_image = divmod(group, TILES_PER_IMAGE // STORE_TILES)
            return group, place, b, group_in_image

        def pooled_cols(n):
            place = place_of(n)[1]
            return slice(place * POOLED_TILE, (place + 1) * POOLED_TILE)

        def rows_step(n):
            row_max[n] = halves_pool.tile([P, M_TILES, N_TILE // 2], F32, name="row_max")
            for m in range(helped(n)):
                nc.vector.tensor_tensor(
                    out=row_max[n][:, m, :].rearrange("p (i x) -> p i x", x=SIDE),
                    in0=acc[(n, m)][:].rearrange("p (i di x) -> p i di x", di=2, x=SIDE)[:, :, 0, :],
                    in1=odd_rows[n][:, m, :].rearrange("p (i x) -> p i x", x=SIDE),
                    op=mybir.AluOpType.max,
                )

        def reduces(n):
            group = place_of(n)[0]
            for m in range(helped(n), M_TILES):
                nc.vector.tensor_reduce(
                    out=pooled[group][:, m, pooled_cols(n)].rearrange("p (i j) -> p i j", j=SIDE // 2),
                    in_=acc[(n, m)][:].rearrange("p (i di j dj) -> p i j di dj", di=2, j=SIDE // 2, dj=2),
                    axis=mybir.AxisListType.XY,
                    op=mybir.AluOpType.max,
                )

        def columns_step(n, first_bank, banks):
            group = place_of(n)[0]
            if banks > 0:
                pairs = row_max[n][:, first_bank : first_bank + banks, :].rearrange("p m (o dj) -> p m o dj", dj=2)
                nc.vector.tensor_tensor(
                    out=pooled[group][:, first_bank : first_bank + banks, pooled_cols(n)],
                    in0=pairs[:, :, :, 0],
                    in1=pairs[:, :, :, 1],
                    op=mybir.AluOpType.max,
                )

        def store(n, half):
            group, place, b, group_in_image = place_of(n)
            store_cols = STORE_TILES * POOLED_TILE
            if place == STORE_TILES - 1:
                nc.sync.dma_start(
                    out=out_views[half][b, :, :, group_in_image * store_cols : (group_in_image + 1) * store_cols],
                    in_=pooled[group][:, 2 * half : 2 * half + 2, :],
                )

        def empty_banks(n):
            group, place = place_of(n)[:2]
            if place == 0:
                pooled[group] = pooled_pool.tile([P, M_TILES, STORE_TILES * POOLED_TILE], F32, name="pooled")
            rows_step(n)
            reduces(n)

        def finish(n):
            columns_step(n, 0, helped(n))
            store(n, 0)
            store(n, 1)

        def load_behind_stores(n):
            if LOAD_TILES <= n and n + LOAD_AHEAD - LOAD_TILES < N_TILES:
                load(n + LOAD_AHEAD - LOAD_TILES, LOAD_TILES)

        regroup(0)
        for n in range(SINGLE_TILES):
            quantise(n)
            multiply(n)
            regroup(n + 1)
            if n == SINGLE_TILES - 1:
                regroup(n + 2)
            if n >= 1:
                copy_odd_rows(n - 1)
                empty_banks(n - 1)
                finish(n - 1)
            if n % LOAD_TILES == 0:
                load_behind_stores(n)
        for a in range(SINGLE_TILES, N_TILES, 2):
            quantise(a)
            multiply(a)
            quantise(a + 1)
            copy_odd_rows(a - 1)
            if a + 2 < N_TILES:
                regroup(a + 2, after=a + 1)
            empty_banks(a - 1)
            multiply(a + 1)
            copy_odd_rows(a)
            if a + 3 < N_TILES:
                regroup(a + 3)
            empty_banks(a)
            finish(a - 1)
            finish(a)
            load_behind_stores(a)
        last = N_TILES - 1
        copy_odd_rows(last)
        rows_step(last)
        for half in range(2):
            columns_step(last, half * M_TILES // 2, M_TILES // 2)
            store(last, half)
